import numpy as np
import ml_dtypes


def mxq(x, axis, fmt="e4m3"):
    dtype, down = {"e4m3": (ml_dtypes.float8_e4m3fn, 7), "e5m2": (ml_dtypes.float8_e5m2, 14)}[fmt]
    v = np.moveaxis(np.asarray(x, np.float32).astype(ml_dtypes.bfloat16).astype(np.float64), axis, -1)
    blocks = v.reshape(v.shape[:-1] + (-1, 32))
    amax = np.abs(blocks).max(-1, keepdims=True)
    byte = np.maximum(np.where(amax > 0, np.frexp(amax)[1] - 1 + 127, 0) - down, 1)
    scale = np.exp2(byte - 127.0)
    codes = (blocks / scale).astype(np.float32).astype(dtype).astype(np.float64)
    return np.moveaxis((codes * scale).reshape(v.shape), -1, axis)


WIDE = False


def mx_kscale(k):
    if not WIDE:
        return np.ones(k)
    levels = np.array([10, -10, 5, -5, 0])
    a = np.random.permutation(np.resize(levels, k // 512 * 4)).reshape(k // 512, 4)
    idx = np.arange(k)
    return np.exp2(a[idx // 512, idx % 128 // 32])


BF16 = ml_dtypes.bfloat16


def bf(x):
    return np.asarray(x, np.float32).astype(BF16)


def f64(x):
    return np.asarray(x).astype(np.float64)


B, V, D, P, Q, R, O = 64, 16, 512, 512, 512, 512, 512
NEG_SLOPE = 0.2


def lrelu(v):
    return np.where(v >= 0, v, NEG_SLOPE * v)


def setup_inputs():
    s, t = mx_kscale(D), mx_kscale(P)
    ss = np.concatenate([s, s])
    return {"F": bf(np.random.standard_normal((B, V, D)) * s),
            "W1": bf(np.random.standard_normal((2 * D, P)) / np.sqrt(2 * D) / ss[:, None] * t),
            "b1": bf(np.random.standard_normal(P) * 0.3 * t),
            "W2": bf(np.random.standard_normal((P, Q)) / np.sqrt(P) / t[:, None]),
            "b2": bf(np.random.standard_normal(Q) * 0.3)}


def reference(F, W1, b1, W2, b2):
    Fq = mxq(f64(F), 2, "e4m3")
    W1 = f64(W1)
    u = Fq @ mxq(W1[:D], 0, "e4m3")
    w = Fq @ mxq(W1[D:], 0, "e4m3")
    h1 = lrelu(u[:, :, None, :] + w[:, None, :, :] + f64(b1))
    return lrelu((mxq(h1, 3, "e4m3") @ mxq(f64(W2), 0, "e4m3")) + f64(b2))

@@ -1,0 +1,263 @@
+from contextlib import ExitStack
+
+import concourse.mybir as mybir
+from concourse.masks import make_identity
+
+F32 = mybir.dt.float32
+BF16 = mybir.dt.bfloat16
+U32 = mybir.dt.uint32
+U8 = mybir.dt.uint8
+FP8X4 = mybir.dt.float8_e4m3fn_x4
+ALU = mybir.AluOpType
+ACT = mybir.ActivationFunctionType
+
+P = 128
+B, V, D, HID, Q = 64, 16, 512, 512, 512
+ROWS1 = B * V
+PAIRS = V * V
+NEG = 0.2
+FLOPS = 2 * ROWS1 * 2 * D * HID + 2 * B * PAIRS * HID * Q
+
+GROUP_B = 2
+N_GROUPS = B // GROUP_B
+CHUNK_B = 8
+GROUPS_PER_CHUNK = CHUNK_B // GROUP_B
+N_CHUNKS = B // CHUNK_B
+V_SHARE = (2, 1)
+
+
+def tile_nonlocalmp_pa_kernel(tc, F, W1, b1, W2, b2, out):
+    nc = tc.nc
+    f_flat = F.flatten_outer_dims()
+    out_flat = out.flatten_outer_dims()
+    with ExitStack() as ctx:
+        ctx.enter_context(tc.manual_schedule())
+        const = ctx.enter_context(tc.tile_pool(name="const", bufs=1))
+        work = ctx.enter_context(tc.tile_pool(name="work", bufs=3))
+        ps_w = ctx.enter_context(tc.psum_pool(name="ps_w", bufs=2))
+        ps_y = ctx.enter_context(tc.psum_pool(name="ps_y", bufs=3))
+        ps_t = ctx.enter_context(tc.psum_pool(name="ps_t", bufs=2))
+
+        w1_raw = const.tile([P, 8, HID], BF16)
+        w1_view = W1.rearrange("(g q e) c -> q g (e c)", g=4, q=P, e=2)
+        w1_dst = w1_raw.rearrange("q (g e) c -> q g (e c)", e=2)
+        f_raw = const.tile([P, 8, D], BF16)
+        f_view = f_flat.rearrange("(n p) d -> p n d", p=P)
+        w2_raw = const.tile([P, 4, Q], BF16)
+        bias_raw = const.tile([P, P], BF16)
+        nc.vector.memset(bias_raw, 0.0)
+        nc.sync.dma_start(out=w1_dst[:, 0:2, :], in_=w1_view[:, 0:2, :])
+        nc.sync.dma_start(out=w1_dst[:, 2:4, :], in_=w1_view[:, 2:4, :])
+        nc.sync.dma_start(out=f_raw[:, 0:2, :], in_=f_view[:, 0:2, :])
+        nc.scalar.dma_start(out=bias_raw[0:4, :], in_=b1.rearrange("(r c) -> r c", c=P))
+        nc.scalar.dma_start(out=bias_raw[4:8, :], in_=b2.rearrange("(r c) -> r c", c=P))
+        nc.sync.dma_start(out=w2_raw, in_=W2.rearrange("(t p) n -> p t n", p=P))
+        nc.sync.dma_start(out=f_raw[:, 2:8, :], in_=f_view[:, 2:8, :])
+
+        ident = const.tile([P, P], F32)
+        make_identity(nc, ident)
+
+        fg = const.tile([P, ROWS1 * 4], BF16, align_bytes=64)
+        fg_w = fg.bitcast(F32).rearrange("p (r u) -> p r u", u=2)
+        f_codes = const.tile([P, ROWS1], U32, align_bytes=64)
+        f_scales = const.tile([P, ROWS1], U8, align_bytes=64)
+        w1g = const.tile([P, 2, HID, 4], BF16, align_bytes=64)
+        w1_codes = const.tile([P, 2 * HID], U32, align_bytes=64)
+        w1_scales = const.tile([P, 2 * HID], U8, align_bytes=64)
+        w2g = const.tile([P, Q, 4], BF16, align_bytes=64)
+        w2_codes = const.tile([P, Q], U32, align_bytes=64)
+        w2_scales = const.tile([P, Q], U8, align_bytes=64)
+        bias_f = const.tile([P, P], F32)
+        bias_sb = const.tile([P, 8], F32)
+        b2_lo = const.tile([P, 4], F32)
+        b2_hi = const.tile([P, 4], F32)
+
+        def f_transpose(pair, on_vector):
+            ft = ps_y.tile([P, 2, 2, P], F32, tag="y")
+            for nn in range(2):
+                words = f_raw[:, 2 * pair + nn, :].bitcast(F32)
+                for u in range(2):
+                    nc.tensor.transpose(ft[:, nn, u, :], words[:, P * u:P * (u + 1)], ident)
+            dst = fg_w[:, 256 * pair:256 * (pair + 1), :].rearrange("p (n r) u -> p n r u", n=2)
+            src = ft.rearrange("p n u r -> p n r u")
+            if on_vector:
+                nc.vector.tensor_copy(out=dst, in_=src)
+            else:
+                nc.scalar.copy(out=dst, in_=src)
+
+        def f_quantise(pair):
+            rows = slice(256 * pair, 256 * (pair + 1))
+            nc.vector.quantize_mx(out=f_codes[:, rows].bitcast(FP8X4), scales=f_scales[:, rows],
+                                  in_=fg[:, 1024 * pair:1024 * (pair + 1)])
+
+        def w1_quantise(h):
+            nc.vector.quantize_mx(
+                out=w1_codes[:, HID * h:HID * (h + 1)].bitcast(FP8X4),
+                scales=w1_scales[:, HID * h:HID * (h + 1)],
+                in_=w1g[:, h].rearrange("q c t -> q (c t)"),
+            )
+
+        nc.vector.tensor_copy(out=w1g[:, 0], in_=w1_raw[:, 0:4, :].rearrange("q t c -> q c t"))
+        nc.scalar.copy(out=w1g[:, 1], in_=w1_raw[:, 4:8, :].rearrange("q t c -> q c t"))
+        nc.vector.tensor_copy(out=bias_f, in_=bias_raw)
+        f_transpose(0, True)
+        w1_quantise(0)
+        bias_ps = ps_y.tile([P, P], F32, tag="y")
+        nc.tensor.transpose(bias_ps, bias_f, ident)
+        f_quantise(0)
+        nc.vector.tensor_copy(out=bias_sb, in_=bias_ps[:, 0:8])
+        nc.vector.tensor_scalar_mul(out=b2_lo, in0=bias_sb[:, 4:8], scalar1=NEG)
+        nc.vector.tensor_scalar_mul(out=b2_hi, in0=bias_sb[:, 4:8], scalar1=1.0 - NEG)
+        w1_quantise(1)
+        nc.scalar.copy(out=w2g, in_=w2_raw.rearrange("p t n -> p n t"))
+
+        b1_bc = bias_sb[:, 0:4].unsqueeze(1).to_broadcast([P, P, 4])
+        u_tiles, w_tiles, ub_tiles = {}, {}, {}
+        a_tiles, h_tiles, code_tiles = {}, {}, {}
+        y_tiles, term_tiles, t_tiles, o_tiles = {}, {}, {}, {}
+
+        def stage1_matmuls(chunk):
+            cols = slice(P * chunk, P * (chunk + 1))
+            ub = ps_w.tile([P, 4, P], F32, tag="u", bufs=1)
+            wb = ps_w.tile([P, 4, P], F32, tag="w")
+            for h, bank in ((0, ub), (1, wb)):
+                for t in range(4):
+                    m = slice(HID * h + P * t, HID * h + P * (t + 1))
+                    nc.tensor.matmul_mx(
+                        out=bank[:, t, :],
+                        lhsT=w1_codes[:, m].bitcast(FP8X4), lhsT_scale=w1_scales[:, m],
+                        rhs=f_codes[:, cols].bitcast(FP8X4), rhs_scale=f_scales[:, cols],
+                        start=True, stop=True,
+                    )
+            ub_tiles[chunk] = ub
+            w_tiles[chunk] = wb
+
+        def stage1_bias(chunk):
+            u_sb = work.tile([P, P, 4], F32, tag="usb", bufs=2)
+            nc.vector.tensor_tensor(out=u_sb, in0=ub_tiles[chunk].rearrange("p t r -> p r t"), in1=b1_bc, op=ALU.add)
+            u_tiles[chunk] = u_sb
+
+        def pair_sum(g, bb):
+            if bb == 0:
+                a_new = work.tile([P, GROUP_B, V, V, 4], F32, tag="a")
+                a_tiles[g] = a_new
+            chunk = g // GROUPS_PER_CHUNK
+            r0 = V * ((g * GROUP_B + bb) % CHUNK_B)
+            nc.vector.tensor_tensor(
+                out=a_tiles[g][:, bb],
+                in0=w_tiles[chunk][:, :, r0:r0 + V].rearrange("p t j -> p j t").unsqueeze(1).to_broadcast([P, V, V, 4]),
+                in1=u_tiles[chunk][:, r0:r0 + V, :].unsqueeze(2).to_broadcast([P, V, V, 4]),
+                op=ALU.add,
+            )
+
+        def hidden_lrelu(g):
+            a_flat = a_tiles[g].rearrange("p b i j t -> p (b i j t)")
+            h_t = work.tile([P, GROUP_B * PAIRS * 4], BF16, tag="h", align_bytes=64)
+            nc.vector.scalar_tensor_tensor(out=h_t, in0=a_flat, scalar=NEG, in1=a_flat, op0=ALU.mult, op1=ALU.max)
+            h_tiles[g] = h_t
+
+        def hidden_quantise(g):
+            h_codes = work.tile([P, GROUP_B * PAIRS], U32, tag="hc", align_bytes=64)
+            h_scales = work.tile([P, GROUP_B * PAIRS], U8, tag="hs", align_bytes=64)
+            nc.vector.quantize_mx(out=h_codes.bitcast(FP8X4), scales=h_scales, in_=h_tiles[g])
+            code_tiles[g] = (h_codes, h_scales)
+
+        def stage2_matmul(g, s):
+            m = slice(P * s, P * (s + 1))
+            h_codes, h_scales = code_tiles[g]
+            y_t = ps_y.tile([P, 512], F32, tag="y")
+            nc.tensor.matmul_mx(
+                out=y_t,
+                lhsT=w2_codes[:, m].bitcast(FP8X4), lhsT_scale=w2_scales[:, m],
+                rhs=h_codes.bitcast(FP8X4), rhs_scale=h_scales,
+                start=True, stop=True,
+            )
+            y_tiles[(g, s)] = y_t
+
+        def output_terms(g, s, on_vector):
+            y_t = y_tiles[(g, s)]
+            p1 = work.tile([P, 512], F32, tag="p1", bufs=8)
+            nc.scalar.activation(out=p1, in_=y_t, func=ACT.Identity, scale=NEG, bias=b2_lo[:, s:s + 1])
+            p2 = work.tile([P, 512], F32, tag="p2", bufs=8)
+            if on_vector:
+                nc.vector.scalar_tensor_tensor(out=p2, in0=y_t, scalar=bias_sb[:, 4 + s:5 + s], in1=p1,
+                                               op0=ALU.add, op1=ALU.max)
+                term_tiles[(g, s)] = (p2,)
+            else:
+                nc.scalar.activation(out=p2, in_=y_t, func=ACT.Relu, scale=1.0 - NEG, bias=b2_hi[:, s:s + 1])
+                term_tiles[(g, s)] = (p1, p2)
+
+        def back_transpose(g, n):
+            tr = ps_t.tile([P, Q], F32, tag="t")
+            c = slice(P * n, P * (n + 1))
+            for s in range(4):
+                m = slice(P * s, P * (s + 1))
+                terms = term_tiles[(g, s)]
+                for k, term in enumerate(terms):
+                    nc.tensor.matmul(out=tr[:, m], lhsT=term[:, c], rhs=ident, is_transpose=True,
+                                     start=(k == 0), stop=(k == len(terms) - 1))
+            t_tiles[(g, n)] = tr
+
+        def copy_out(g, n, on_vector):
+            if n == 0:
+                o_new = work.tile([P, 4, Q], F32, tag="o")
+                o_tiles[g] = o_new
+            if on_vector:
+                nc.vector.tensor_copy(out=o_tiles[g][:, n, :], in_=t_tiles[(g, n)])
+            else:
+                nc.scalar.copy(out=o_tiles[g][:, n, :], in_=t_tiles[(g, n)])
+
+        def store(g, n0, n1):
+            nc.sync.dma_start(
+                out=out_flat[512 * g + P * n0:512 * g + P * n1, :].rearrange("(n p) q -> p n q", p=P),
+                in_=o_tiles[g][:, n0:n1, :],
+            )
+
+        stage1_matmuls(0)
+        stage1_bias(0)
+
+        for it in range(N_GROUPS + 2):
+            g_h, g_y, g_t = it, it - 1, it - 2
+            have_h = g_h < N_GROUPS
+            have_y = 0 <= g_y < N_GROUPS
+            have_t = 0 <= g_t
+            if have_h:
+                pair_sum(g_h, 0)
+                pair_sum(g_h, 1)
+                hidden_lrelu(g_h)
+                share = V_SHARE[it % len(V_SHARE)]
+            else:
+                share = 4
+            for half in range(2):
+                qs = (2 * half, 2 * half + 1)
+                if have_t:
+                    for q in qs:
+                        back_transpose(g_t, q)
+                if have_y:
+                    for q in qs:
+                        stage2_matmul(g_y, q)
+                for q in qs:
+                    if have_t:
+                        copy_out(g_t, q, (not have_h) and q % 2 == 1)
+                        if g_t == N_GROUPS - 1:
+                            store(g_t, q, q + 1)
+                    if have_y:
+                        output_terms(g_y, q, q >= 4 - share)
+            if have_t and g_t < N_GROUPS - 1:
+                store(g_t, 0, 4)
+            if it == 0:
+                nc.vector.quantize_mx(out=w2_codes.bitcast(FP8X4), scales=w2_scales,
+                                      in_=w2g.rearrange("p n t -> p (n t)"))
+                f_transpose(1, False)
+            if it in (1, 2):
+                f_quantise(it)
+                f_transpose(it + 1, False)
+            if it == 3:
+                f_quantise(3)
+            nxt = it // GROUPS_PER_CHUNK + 1
+            if nxt < N_CHUNKS and it % GROUPS_PER_CHUNK == 2:
+                stage1_matmuls(nxt)
+            if nxt < N_CHUNKS and it % GROUPS_PER_CHUNK == 3:
+                stage1_bias(nxt)
+            if have_h:
+                hidden_quantise(g_h)

@@ -23,7 +23,7 @@ N_GROUPS = B // GROUP_B
 CHUNK_B = 8
 GROUPS_PER_CHUNK = CHUNK_B // GROUP_B
 N_CHUNKS = B // CHUNK_B
-V_SHARE = (2, 1)
+RATIO = 1.0 / NEG - 1.0
 
 
 def tile_nonlocalmp_pa_kernel(tc, F, W1, b1, W2, b2, out):
@@ -174,18 +174,21 @@ def tile_nonlocalmp_pa_kernel(tc, F, W1, b1, W2, b2, out):
             )
             y_tiles[(g, s)] = y_t
 
-        def output_terms(g, s, on_vector):
-            y_t = y_tiles[(g, s)]
-            p1 = work.tile([P, 512], F32, tag="p1", bufs=8)
-            nc.scalar.activation(out=p1, in_=y_t, func=ACT.Identity, scale=NEG, bias=b2_lo[:, s:s + 1])
-            p2 = work.tile([P, 512], F32, tag="p2", bufs=8)
-            if on_vector:
-                nc.vector.scalar_tensor_tensor(out=p2, in0=y_t, scalar=bias_sb[:, 4 + s:5 + s], in1=p1,
-                                               op0=ALU.add, op1=ALU.max)
-                term_tiles[(g, s)] = (p2,)
-            else:
-                nc.scalar.activation(out=p2, in_=y_t, func=ACT.Relu, scale=1.0 - NEG, bias=b2_hi[:, s:s + 1])
-                term_tiles[(g, s)] = (p1, p2)
+        def output_terms(g, half, last):
+            p1 = work.tile([P, 2, 512], F32, tag="p1", bufs=6)
+            p2 = work.tile([P, 2, 512], F32, tag="p2", bufs=6)
+            for k in range(2):
+                s = 2 * half + k
+                y_t = y_tiles[(g, s)]
+                nc.scalar.activation(out=p1[:, k, :], in_=y_t, func=ACT.Identity, scale=NEG, bias=b2_lo[:, s:s + 1])
+                if last:
+                    nc.vector.scalar_tensor_tensor(out=p2[:, k, :], in0=y_t, scalar=bias_sb[:, 4 + s:5 + s],
+                                                   in1=p1[:, k, :], op0=ALU.add, op1=ALU.max)
+                    term_tiles[(g, s)] = (p2[:, k, :],)
+                else:
+                    term_tiles[(g, s)] = (p1[:, k, :], p2[:, k, :])
+            if not last:
+                nc.gpsimd.tensor_scalar(out=p2, in0=p1, scalar1=RATIO, scalar2=0.0, op0=ALU.mult, op1=ALU.max)
 
         def back_transpose(g, n):
             tr = ps_t.tile([P, Q], F32, tag="t")
@@ -216,18 +219,26 @@ def tile_nonlocalmp_pa_kernel(tc, F, W1, b1, W2, b2, out):
         stage1_matmuls(0)
         stage1_bias(0)
 
-        for it in range(N_GROUPS + 2):
-            g_h, g_y, g_t = it, it - 1, it - 2
+        for it in range(N_GROUPS + 3):
+            g_h, g_y, g_t = it, it - 1, it - 3
             have_h = g_h < N_GROUPS
             have_y = 0 <= g_y < N_GROUPS
             have_t = 0 <= g_t
+            nxt = it // GROUPS_PER_CHUNK + 1
             if have_h:
                 pair_sum(g_h, 0)
+            if it == 0:
+                nc.vector.quantize_mx(out=w2_codes.bitcast(FP8X4), scales=w2_scales,
+                                      in_=w2g.rearrange("p n t -> p (n t)"))
+            if have_y:
+                hidden_quantise(g_y)
+            if have_h:
                 pair_sum(g_h, 1)
+                if it in (1, 2, 3):
+                    f_quantise(it)
+                if nxt < N_CHUNKS and it % GROUPS_PER_CHUNK == 2:
+                    stage1_bias(nxt)
                 hidden_lrelu(g_h)
-                share = V_SHARE[it % len(V_SHARE)]
-            else:
-                share = 4
             for half in range(2):
                 qs = (2 * half, 2 * half + 1)
                 if have_t:
@@ -236,28 +247,16 @@ def tile_nonlocalmp_pa_kernel(tc, F, W1, b1, W2, b2, out):
                 if have_y:
                     for q in qs:
                         stage2_matmul(g_y, q)
-                for q in qs:
-                    if have_t:
+                if have_t:
+                    for q in qs:
                         copy_out(g_t, q, (not have_h) and q % 2 == 1)
-                        if g_t == N_GROUPS - 1:
+                        if g_t >= N_GROUPS - 2:
                             store(g_t, q, q + 1)
-                    if have_y:
-                        output_terms(g_y, q, q >= 4 - share)
-            if have_t and g_t < N_GROUPS - 1:
+                if have_y:
+                    output_terms(g_y, half, g_y == N_GROUPS - 1)
+            if have_t and g_t < N_GROUPS - 2:
                 store(g_t, 0, 4)
-            if it == 0:
-                nc.vector.quantize_mx(out=w2_codes.bitcast(FP8X4), scales=w2_scales,
-                                      in_=w2g.rearrange("p n t -> p (n t)"))
-                f_transpose(1, False)
-            if it in (1, 2):
-                f_quantise(it)
-                f_transpose(it + 1, False)
-            if it == 3:
-                f_quantise(3)
-            nxt = it // GROUPS_PER_CHUNK + 1
-            if nxt < N_CHUNKS and it % GROUPS_PER_CHUNK == 2:
+            if nxt < N_CHUNKS and it % GROUPS_PER_CHUNK == 1:
                 stage1_matmuls(nxt)
-            if nxt < N_CHUNKS and it % GROUPS_PER_CHUNK == 3:
-                stage1_bias(nxt)
-            if have_h:
-                hidden_quantise(g_h)
+            if it in (0, 1, 2):
+                f_transpose(it + 1, False)

@@ -23,7 +23,7 @@ N_GROUPS = B // GROUP_B
 CHUNK_B = 8
 GROUPS_PER_CHUNK = CHUNK_B // GROUP_B
 N_CHUNKS = B // CHUNK_B
-RATIO = 1.0 / NEG - 1.0
+V_SHARE = (1, 2, 1)
 
 
 def tile_nonlocalmp_pa_kernel(tc, F, W1, b1, W2, b2, out):
@@ -34,9 +34,9 @@ def tile_nonlocalmp_pa_kernel(tc, F, W1, b1, W2, b2, out):
         ctx.enter_context(tc.manual_schedule())
         const = ctx.enter_context(tc.tile_pool(name="const", bufs=1))
         work = ctx.enter_context(tc.tile_pool(name="work", bufs=3))
-        ps_w = ctx.enter_context(tc.psum_pool(name="ps_w", bufs=2))
-        ps_y = ctx.enter_context(tc.psum_pool(name="ps_y", bufs=3))
-        ps_t = ctx.enter_context(tc.psum_pool(name="ps_t", bufs=2))
+        ps_s = ctx.enter_context(tc.psum_pool(name="ps_s", bufs=1))
+        ps_y = ctx.enter_context(tc.psum_pool(name="ps_y", bufs=4))
+        ps_t = ctx.enter_context(tc.psum_pool(name="ps_t", bufs=3))
 
         w1_raw = const.tile([P, 8, HID], BF16)
         w1_view = W1.rearrange("(g q e) c -> q g (e c)", g=4, q=P, e=2)
@@ -72,8 +72,8 @@ def tile_nonlocalmp_pa_kernel(tc, F, W1, b1, W2, b2, out):
         b2_lo = const.tile([P, 4], F32)
         b2_hi = const.tile([P, 4], F32)
 
-        def f_transpose(pair, on_vector):
-            ft = ps_y.tile([P, 2, 2, P], F32, tag="y")
+        def f_transpose(pair, pool, tag, on_vector):
+            ft = pool.tile([P, 2, 2, P], F32, tag=tag)
             for nn in range(2):
                 words = f_raw[:, 2 * pair + nn, :].bitcast(F32)
                 for u in range(2):
@@ -97,45 +97,34 @@ def tile_nonlocalmp_pa_kernel(tc, F, W1, b1, W2, b2, out):
                 in_=w1g[:, h].rearrange("q c t -> q (c t)"),
             )
 
-        nc.vector.tensor_copy(out=w1g[:, 0], in_=w1_raw[:, 0:4, :].rearrange("q t c -> q c t"))
-        nc.scalar.copy(out=w1g[:, 1], in_=w1_raw[:, 4:8, :].rearrange("q t c -> q c t"))
-        nc.vector.tensor_copy(out=bias_f, in_=bias_raw)
-        f_transpose(0, True)
-        w1_quantise(0)
-        bias_ps = ps_y.tile([P, P], F32, tag="y")
-        nc.tensor.transpose(bias_ps, bias_f, ident)
-        f_quantise(0)
-        nc.vector.tensor_copy(out=bias_sb, in_=bias_ps[:, 0:8])
-        nc.vector.tensor_scalar_mul(out=b2_lo, in0=bias_sb[:, 4:8], scalar1=NEG)
-        nc.vector.tensor_scalar_mul(out=b2_hi, in0=bias_sb[:, 4:8], scalar1=1.0 - NEG)
-        w1_quantise(1)
-        nc.scalar.copy(out=w2g, in_=w2_raw.rearrange("p t n -> p n t"))
-
         b1_bc = bias_sb[:, 0:4].unsqueeze(1).to_broadcast([P, P, 4])
-        u_tiles, w_tiles, ub_tiles = {}, {}, {}
+        s1_banks, u_tiles, w_tiles = {}, {}, {}
         a_tiles, h_tiles, code_tiles = {}, {}, {}
         y_tiles, term_tiles, t_tiles, o_tiles = {}, {}, {}, {}
 
-        def stage1_matmuls(chunk):
+        def stage1_matmuls(chunk, h, pool, tag):
             cols = slice(P * chunk, P * (chunk + 1))
-            ub = ps_w.tile([P, 4, P], F32, tag="u", bufs=1)
-            wb = ps_w.tile([P, 4, P], F32, tag="w")
-            for h, bank in ((0, ub), (1, wb)):
-                for t in range(4):
-                    m = slice(HID * h + P * t, HID * h + P * (t + 1))
-                    nc.tensor.matmul_mx(
-                        out=bank[:, t, :],
-                        lhsT=w1_codes[:, m].bitcast(FP8X4), lhsT_scale=w1_scales[:, m],
-                        rhs=f_codes[:, cols].bitcast(FP8X4), rhs_scale=f_scales[:, cols],
-                        start=True, stop=True,
-                    )
-            ub_tiles[chunk] = ub
-            w_tiles[chunk] = wb
+            bank = pool.tile([P, 4, P], F32, tag=tag)
+            for t in range(4):
+                m = slice(HID * h + P * t, HID * h + P * (t + 1))
+                nc.tensor.matmul_mx(
+                    out=bank[:, t, :],
+                    lhsT=w1_codes[:, m].bitcast(FP8X4), lhsT_scale=w1_scales[:, m],
+                    rhs=f_codes[:, cols].bitcast(FP8X4), rhs_scale=f_scales[:, cols],
+                    start=True, stop=True,
+                )
+            s1_banks[(chunk, h)] = bank
 
-        def stage1_bias(chunk):
+        def stage1_u(chunk):
             u_sb = work.tile([P, P, 4], F32, tag="usb", bufs=2)
-            nc.vector.tensor_tensor(out=u_sb, in0=ub_tiles[chunk].rearrange("p t r -> p r t"), in1=b1_bc, op=ALU.add)
+            nc.vector.tensor_tensor(out=u_sb, in0=s1_banks[(chunk, 0)].rearrange("p t r -> p r t"), in1=b1_bc,
+                                    op=ALU.add)
             u_tiles[chunk] = u_sb
+
+        def stage1_w(chunk):
+            w_sb = work.tile([P, P, 4], F32, tag="wsb", bufs=2)
+            nc.scalar.copy(out=w_sb, in_=s1_banks[(chunk, 1)].rearrange("p t r -> p r t"))
+            w_tiles[chunk] = w_sb
 
         def pair_sum(g, bb):
             if bb == 0:
@@ -145,7 +134,7 @@ def tile_nonlocalmp_pa_kernel(tc, F, W1, b1, W2, b2, out):
             r0 = V * ((g * GROUP_B + bb) % CHUNK_B)
             nc.vector.tensor_tensor(
                 out=a_tiles[g][:, bb],
-                in0=w_tiles[chunk][:, :, r0:r0 + V].rearrange("p t j -> p j t").unsqueeze(1).to_broadcast([P, V, V, 4]),
+                in0=w_tiles[chunk][:, r0:r0 + V, :].unsqueeze(1).to_broadcast([P, V, V, 4]),
                 in1=u_tiles[chunk][:, r0:r0 + V, :].unsqueeze(2).to_broadcast([P, V, V, 4]),
                 op=ALU.add,
             )
@@ -174,21 +163,18 @@ def tile_nonlocalmp_pa_kernel(tc, F, W1, b1, W2, b2, out):
             )
             y_tiles[(g, s)] = y_t
 
-        def output_terms(g, half, last):
-            p1 = work.tile([P, 2, 512], F32, tag="p1", bufs=6)
-            p2 = work.tile([P, 2, 512], F32, tag="p2", bufs=6)
-            for k in range(2):
-                s = 2 * half + k
-                y_t = y_tiles[(g, s)]
-                nc.scalar.activation(out=p1[:, k, :], in_=y_t, func=ACT.Identity, scale=NEG, bias=b2_lo[:, s:s + 1])
-                if last:
-                    nc.vector.scalar_tensor_tensor(out=p2[:, k, :], in0=y_t, scalar=bias_sb[:, 4 + s:5 + s],
-                                                   in1=p1[:, k, :], op0=ALU.add, op1=ALU.max)
-                    term_tiles[(g, s)] = (p2[:, k, :],)
-                else:
-                    term_tiles[(g, s)] = (p1[:, k, :], p2[:, k, :])
-            if not last:
-                nc.gpsimd.tensor_scalar(out=p2, in0=p1, scalar1=RATIO, scalar2=0.0, op0=ALU.mult, op1=ALU.max)
+        def output_terms(g, s, on_vector):
+            y_t = y_tiles[(g, s)]
+            p1 = work.tile([P, 512], F32, tag="p1", bufs=8)
+            nc.scalar.activation(out=p1, in_=y_t, func=ACT.Identity, scale=NEG, bias=b2_lo[:, s:s + 1])
+            p2 = work.tile([P, 512], F32, tag="p2", bufs=8)
+            if on_vector:
+                nc.vector.scalar_tensor_tensor(out=p2, in0=y_t, scalar=bias_sb[:, 4 + s:5 + s], in1=p1,
+                                               op0=ALU.add, op1=ALU.max)
+                term_tiles[(g, s)] = (p2,)
+            else:
+                nc.scalar.activation(out=p2, in_=y_t, func=ACT.Relu, scale=1.0 - NEG, bias=b2_hi[:, s:s + 1])
+                term_tiles[(g, s)] = (p1, p2)
 
         def back_transpose(g, n):
             tr = ps_t.tile([P, Q], F32, tag="t")
@@ -216,15 +202,33 @@ def tile_nonlocalmp_pa_kernel(tc, F, W1, b1, W2, b2, out):
                 in_=o_tiles[g][:, n0:n1, :],
             )
 
-        stage1_matmuls(0)
-        stage1_bias(0)
+        nc.vector.tensor_copy(out=w1g[:, 0], in_=w1_raw[:, 0:4, :].rearrange("q t c -> q c t"))
+        nc.scalar.copy(out=w1g[:, 1], in_=w1_raw[:, 4:8, :].rearrange("q t c -> q c t"))
+        nc.vector.tensor_copy(out=bias_f, in_=bias_raw)
+        f_transpose(0, ps_y, "y", True)
+        w1_quantise(0)
+        bias_ps = ps_y.tile([P, P], F32, tag="y")
+        nc.tensor.transpose(bias_ps, bias_f, ident)
+        f_quantise(0)
+        nc.vector.tensor_copy(out=bias_sb, in_=bias_ps[:, 0:8])
+        stage1_matmuls(0, 0, ps_y, "y")
+        w1_quantise(1)
+        stage1_matmuls(0, 1, ps_y, "y")
+        stage1_u(0)
+        stage1_w(0)
+        nc.vector.tensor_scalar_mul(out=b2_lo, in0=bias_sb[:, 4:8], scalar1=NEG)
+        nc.vector.tensor_scalar_mul(out=b2_hi, in0=bias_sb[:, 4:8], scalar1=1.0 - NEG)
+        nc.scalar.copy(out=w2g, in_=w2_raw.rearrange("p t n -> p n t"))
+        for pair in (1, 2, 3):
+            f_transpose(pair, ps_t, "t", False)
 
-        for it in range(N_GROUPS + 3):
-            g_h, g_y, g_t = it, it - 1, it - 3
+        for it in range(N_GROUPS + 2):
+            g_h, g_y, g_t = it, it - 1, it - 2
             have_h = g_h < N_GROUPS
             have_y = 0 <= g_y < N_GROUPS
             have_t = 0 <= g_t
             nxt = it // GROUPS_PER_CHUNK + 1
+            phase = it % GROUPS_PER_CHUNK
             if have_h:
                 pair_sum(g_h, 0)
             if it == 0:
@@ -236,27 +240,27 @@ def tile_nonlocalmp_pa_kernel(tc, F, W1, b1, W2, b2, out):
                 pair_sum(g_h, 1)
                 if it in (1, 2, 3):
                     f_quantise(it)
-                if nxt < N_CHUNKS and it % GROUPS_PER_CHUNK == 2:
-                    stage1_bias(nxt)
+                if nxt < N_CHUNKS and phase == 2:
+                    stage1_u(nxt)
                 hidden_lrelu(g_h)
-            for half in range(2):
-                qs = (2 * half, 2 * half + 1)
-                if have_t:
-                    for q in qs:
-                        back_transpose(g_t, q)
-                if have_y:
-                    for q in qs:
-                        stage2_matmul(g_y, q)
-                if have_t:
-                    for q in qs:
-                        copy_out(g_t, q, (not have_h) and q % 2 == 1)
-                        if g_t >= N_GROUPS - 2:
-                            store(g_t, q, q + 1)
-                if have_y:
-                    output_terms(g_y, half, g_y == N_GROUPS - 1)
-            if have_t and g_t < N_GROUPS - 2:
-                store(g_t, 0, 4)
-            if nxt < N_CHUNKS and it % GROUPS_PER_CHUNK == 1:
-                stage1_matmuls(nxt)
-            if it in (0, 1, 2):
-                f_transpose(it + 1, False)
+                share = V_SHARE[it % len(V_SHARE)]
+            else:
+                share = 4
+            if nxt < N_CHUNKS and phase == 3:
+                stage1_w(nxt)
+            if have_y:
+                for s in range(4):
+                    stage2_matmul(g_y, s)
+                for s in range(4):
+                    output_terms(g_y, s, s < share)
+            if have_t:
+                for n in range(4):
+                    back_transpose(g_t, n)
+                for n in range(4):
+                    copy_out(g_t, n, (not have_h) and n % 2 == 1)
+                    if g_t >= N_GROUPS - 2:
+                        store(g_t, n, n + 1)
+                if g_t < N_GROUPS - 2:
+                    store(g_t, 0, 4)
+            if nxt < N_CHUNKS and phase in (1, 2):
+                stage1_matmuls(nxt, phase - 1, ps_s, "s1")

@@ -23,7 +23,7 @@ N_GROUPS = B // GROUP_B
 CHUNK_B = 8
 GROUPS_PER_CHUNK = CHUNK_B // GROUP_B
 N_CHUNKS = B // CHUNK_B
-V_SHARE = (1, 2, 1)
+N_E_VECTOR = 2
 
 
 def tile_nonlocalmp_pa_kernel(tc, F, W1, b1, W2, b2, out):
@@ -34,9 +34,8 @@ def tile_nonlocalmp_pa_kernel(tc, F, W1, b1, W2, b2, out):
         ctx.enter_context(tc.manual_schedule())
         const = ctx.enter_context(tc.tile_pool(name="const", bufs=1))
         work = ctx.enter_context(tc.tile_pool(name="work", bufs=3))
-        ps_s = ctx.enter_context(tc.psum_pool(name="ps_s", bufs=1))
         ps_y = ctx.enter_context(tc.psum_pool(name="ps_y", bufs=4))
-        ps_t = ctx.enter_context(tc.psum_pool(name="ps_t", bufs=3))
+        ps_t = ctx.enter_context(tc.psum_pool(name="ps_t", bufs=4))
 
         w1_raw = const.tile([P, 8, HID], BF16)
         w1_view = W1.rearrange("(g q e) c -> q g (e c)", g=4, q=P, e=2)
@@ -69,8 +68,7 @@ def tile_nonlocalmp_pa_kernel(tc, F, W1, b1, W2, b2, out):
         w2_scales = const.tile([P, Q], U8, align_bytes=64)
         bias_f = const.tile([P, P], F32)
         bias_sb = const.tile([P, 8], F32)
-        b2_lo = const.tile([P, 4], F32)
-        b2_hi = const.tile([P, 4], F32)
+        b2_neg = const.tile([P, 4], F32)
 
         def f_transpose(pair, pool, tag, on_vector):
             ft = pool.tile([P, 2, 2, P], F32, tag=tag)
@@ -100,7 +98,7 @@ def tile_nonlocalmp_pa_kernel(tc, F, W1, b1, W2, b2, out):
         b1_bc = bias_sb[:, 0:4].unsqueeze(1).to_broadcast([P, P, 4])
         s1_banks, u_tiles, w_tiles = {}, {}, {}
         a_tiles, h_tiles, code_tiles = {}, {}, {}
-        y_tiles, term_tiles, t_tiles, o_tiles = {}, {}, {}, {}
+        y_tiles, z_tiles, e_tiles, t_tiles, o_tiles = {}, {}, {}, {}, {}
 
         def stage1_matmuls(chunk, h, pool, tag):
             cols = slice(P * chunk, P * (chunk + 1))
@@ -163,28 +161,32 @@ def tile_nonlocalmp_pa_kernel(tc, F, W1, b1, W2, b2, out):
             )
             y_tiles[(g, s)] = y_t
 
-        def output_terms(g, s, on_vector):
+        def output_z(g, s, scalar_makes_e):
+            if s == 0:
+                z_new = work.tile([P, 4, 512], F32, tag="z")
+                e_new = work.tile([P, 4, 512], F32, tag="e")
+                z_tiles[g] = z_new
+                e_tiles[g] = e_new
             y_t = y_tiles[(g, s)]
-            p1 = work.tile([P, 512], F32, tag="p1", bufs=8)
-            nc.scalar.activation(out=p1, in_=y_t, func=ACT.Identity, scale=NEG, bias=b2_lo[:, s:s + 1])
-            p2 = work.tile([P, 512], F32, tag="p2", bufs=8)
-            if on_vector:
-                nc.vector.scalar_tensor_tensor(out=p2, in0=y_t, scalar=bias_sb[:, 4 + s:5 + s], in1=p1,
-                                               op0=ALU.add, op1=ALU.max)
-                term_tiles[(g, s)] = (p2,)
-            else:
-                nc.scalar.activation(out=p2, in_=y_t, func=ACT.Relu, scale=1.0 - NEG, bias=b2_hi[:, s:s + 1])
-                term_tiles[(g, s)] = (p1, p2)
+            nc.scalar.activation(out=z_tiles[g][:, s, :], in_=y_t, func=ACT.Identity, scale=1.0,
+                                 bias=bias_sb[:, 4 + s:5 + s])
+            if scalar_makes_e:
+                nc.scalar.activation(out=e_tiles[g][:, s, :], in_=y_t, func=ACT.Relu, scale=NEG - 1.0,
+                                     bias=b2_neg[:, s:s + 1])
+
+        def vector_e(g, n_slices):
+            nc.vector.tensor_scalar(out=e_tiles[g][:, 0:n_slices, :], in0=z_tiles[g][:, 0:n_slices, :],
+                                    scalar1=NEG - 1.0, scalar2=0.0, op0=ALU.mult, op1=ALU.max)
 
         def back_transpose(g, n):
             tr = ps_t.tile([P, Q], F32, tag="t")
             c = slice(P * n, P * (n + 1))
             for s in range(4):
                 m = slice(P * s, P * (s + 1))
-                terms = term_tiles[(g, s)]
-                for k, term in enumerate(terms):
-                    nc.tensor.matmul(out=tr[:, m], lhsT=term[:, c], rhs=ident, is_transpose=True,
-                                     start=(k == 0), stop=(k == len(terms) - 1))
+                nc.tensor.matmul(out=tr[:, m], lhsT=z_tiles[g][:, s, c], rhs=ident, is_transpose=True,
+                                 start=True, stop=False)
+                nc.tensor.matmul(out=tr[:, m], lhsT=e_tiles[g][:, s, c], rhs=ident, is_transpose=True,
+                                 start=False, stop=True)
             t_tiles[(g, n)] = tr
 
         def copy_out(g, n, on_vector):
@@ -216,8 +218,7 @@ def tile_nonlocalmp_pa_kernel(tc, F, W1, b1, W2, b2, out):
         stage1_matmuls(0, 1, ps_y, "y")
         stage1_u(0)
         stage1_w(0)
-        nc.vector.tensor_scalar_mul(out=b2_lo, in0=bias_sb[:, 4:8], scalar1=NEG)
-        nc.vector.tensor_scalar_mul(out=b2_hi, in0=bias_sb[:, 4:8], scalar1=1.0 - NEG)
+        nc.vector.tensor_scalar_mul(out=b2_neg, in0=bias_sb[:, 4:8], scalar1=NEG - 1.0)
         nc.scalar.copy(out=w2g, in_=w2_raw.rearrange("p t n -> p n t"))
         for pair in (1, 2, 3):
             f_transpose(pair, ps_t, "t", False)
@@ -229,30 +230,35 @@ def tile_nonlocalmp_pa_kernel(tc, F, W1, b1, W2, b2, out):
             have_t = 0 <= g_t
             nxt = it // GROUPS_PER_CHUNK + 1
             phase = it % GROUPS_PER_CHUNK
+            prefetch = nxt < N_CHUNKS
             if have_h:
                 pair_sum(g_h, 0)
+            if prefetch and phase == 2:
+                stage1_u(nxt)
+            if have_t:
+                vector_e(g_t, N_E_VECTOR)
+            if have_h:
+                pair_sum(g_h, 1)
+            if have_y and g_y > 0:
+                hidden_quantise(g_y)
+            if it in (1, 2, 3):
+                f_quantise(it)
+            if have_h:
+                hidden_lrelu(g_h)
             if it == 0:
                 nc.vector.quantize_mx(out=w2_codes.bitcast(FP8X4), scales=w2_scales,
                                       in_=w2g.rearrange("p n t -> p (n t)"))
-            if have_y:
-                hidden_quantise(g_y)
-            if have_h:
-                pair_sum(g_h, 1)
-                if it in (1, 2, 3):
-                    f_quantise(it)
-                if nxt < N_CHUNKS and phase == 2:
-                    stage1_u(nxt)
-                hidden_lrelu(g_h)
-                share = V_SHARE[it % len(V_SHARE)]
-            else:
-                share = 4
-            if nxt < N_CHUNKS and phase == 3:
+                hidden_quantise(0)
+            if prefetch and phase == 2:
                 stage1_w(nxt)
             if have_y:
                 for s in range(4):
                     stage2_matmul(g_y, s)
                 for s in range(4):
-                    output_terms(g_y, s, s < share)
+                    output_z(g_y, s, s >= N_E_VECTOR)
+            if prefetch and phase == 1:
+                stage1_matmuls(nxt, 0, ps_y, "y")
+                stage1_matmuls(nxt, 1, ps_y, "y")
             if have_t:
                 for n in range(4):
                     back_transpose(g_t, n)
@@ -262,5 +268,3 @@ def tile_nonlocalmp_pa_kernel(tc, F, W1, b1, W2, b2, out):
                         store(g_t, n, n + 1)
                 if g_t < N_GROUPS - 2:
                     store(g_t, 0, 4)
-            if nxt < N_CHUNKS and phase in (1, 2):
-                stage1_matmuls(nxt, phase - 1, ps_s, "s1")

@@ -23,6 +23,8 @@ N_GROUPS = B // GROUP_B
 CHUNK_B = 8
 GROUPS_PER_CHUNK = CHUNK_B // GROUP_B
 N_CHUNKS = B // CHUNK_B
+FIRST_SINGLE = N_GROUPS - 2
+V_COLS = 320
 N_E_VECTOR = 2
 
 
@@ -45,9 +47,9 @@ def tile_nonlocalmp_pa_kernel(tc, F, W1, b1, W2, b2, out):
         w2_raw = const.tile([P, 4, Q], BF16)
         bias_raw = const.tile([P, P], BF16)
         nc.vector.memset(bias_raw, 0.0)
+        nc.sync.dma_start(out=f_raw[:, 0:2, :], in_=f_view[:, 0:2, :])
         nc.sync.dma_start(out=w1_dst[:, 0:2, :], in_=w1_view[:, 0:2, :])
         nc.sync.dma_start(out=w1_dst[:, 2:4, :], in_=w1_view[:, 2:4, :])
-        nc.sync.dma_start(out=f_raw[:, 0:2, :], in_=f_view[:, 0:2, :])
         nc.scalar.dma_start(out=bias_raw[0:4, :], in_=b1.rearrange("(r c) -> r c", c=P))
         nc.scalar.dma_start(out=bias_raw[4:8, :], in_=b2.rearrange("(r c) -> r c", c=P))
         nc.sync.dma_start(out=w2_raw, in_=W2.rearrange("(t p) n -> p t n", p=P))
@@ -124,16 +126,17 @@ def tile_nonlocalmp_pa_kernel(tc, F, W1, b1, W2, b2, out):
             nc.scalar.copy(out=w_sb, in_=s1_banks[(chunk, 1)].rearrange("p t r -> p r t"))
             w_tiles[chunk] = w_sb
 
-        def pair_sum(g, bb):
-            if bb == 0:
-                a_new = work.tile([P, GROUP_B, V, V, 4], F32, tag="a")
-                a_tiles[g] = a_new
+        def pair_sum(g):
+            a_new = work.tile([P, GROUP_B, V, V, 4], F32, tag="a")
+            a_tiles[g] = a_new
             chunk = g // GROUPS_PER_CHUNK
-            r0 = V * ((g * GROUP_B + bb) % CHUNK_B)
+            r0 = V * ((g * GROUP_B) % CHUNK_B)
+            rows = slice(r0, r0 + GROUP_B * V)
+            full = [P, GROUP_B, V, V, 4]
             nc.vector.tensor_tensor(
-                out=a_tiles[g][:, bb],
-                in0=w_tiles[chunk][:, r0:r0 + V, :].unsqueeze(1).to_broadcast([P, V, V, 4]),
-                in1=u_tiles[chunk][:, r0:r0 + V, :].unsqueeze(2).to_broadcast([P, V, V, 4]),
+                out=a_new,
+                in0=w_tiles[chunk][:, rows, :].rearrange("p (b j) t -> p b j t", b=GROUP_B).unsqueeze(2).to_broadcast(full),
+                in1=u_tiles[chunk][:, rows, :].rearrange("p (b i) t -> p b i t", b=GROUP_B).unsqueeze(3).to_broadcast(full),
                 op=ALU.add,
             )
 
@@ -174,6 +177,11 @@ def tile_nonlocalmp_pa_kernel(tc, F, W1, b1, W2, b2, out):
                 nc.scalar.activation(out=e_tiles[g][:, s, :], in_=y_t, func=ACT.Relu, scale=NEG - 1.0,
                                      bias=b2_neg[:, s:s + 1])
 
+        def vector_lrelu(g, s):
+            z_s = z_tiles[g][:, s, :]
+            nc.vector.scalar_tensor_tensor(out=e_tiles[g][:, s, :], in0=z_s, scalar=NEG, in1=z_s,
+                                           op0=ALU.mult, op1=ALU.max)
+
         def vector_e(g, n_slices):
             nc.vector.tensor_scalar(out=e_tiles[g][:, 0:n_slices, :], in0=z_tiles[g][:, 0:n_slices, :],
                                     scalar1=NEG - 1.0, scalar2=0.0, op0=ALU.mult, op1=ALU.max)
@@ -183,10 +191,11 @@ def tile_nonlocalmp_pa_kernel(tc, F, W1, b1, W2, b2, out):
             c = slice(P * n, P * (n + 1))
             for s in range(4):
                 m = slice(P * s, P * (s + 1))
-                nc.tensor.matmul(out=tr[:, m], lhsT=z_tiles[g][:, s, c], rhs=ident, is_transpose=True,
-                                 start=True, stop=False)
+                if g < FIRST_SINGLE:
+                    nc.tensor.matmul(out=tr[:, m], lhsT=z_tiles[g][:, s, c], rhs=ident, is_transpose=True,
+                                     start=True, stop=False)
                 nc.tensor.matmul(out=tr[:, m], lhsT=e_tiles[g][:, s, c], rhs=ident, is_transpose=True,
-                                 start=False, stop=True)
+                                 start=(g >= FIRST_SINGLE), stop=True)
             t_tiles[(g, n)] = tr
 
         def copy_out(g, n, on_vector):
@@ -204,21 +213,26 @@ def tile_nonlocalmp_pa_kernel(tc, F, W1, b1, W2, b2, out):
                 in_=o_tiles[g][:, n0:n1, :],
             )
 
-        nc.vector.tensor_copy(out=w1g[:, 0], in_=w1_raw[:, 0:4, :].rearrange("q t c -> q c t"))
-        nc.scalar.copy(out=w1g[:, 1], in_=w1_raw[:, 4:8, :].rearrange("q t c -> q c t"))
+        def w1_regroup(h):
+            src = w1_raw[:, 4 * h:4 * h + 4, :].rearrange("q t c -> q c t")
+            nc.vector.tensor_copy(out=w1g[:, h, 0:V_COLS, :], in_=src[:, 0:V_COLS, :])
+            nc.scalar.copy(out=w1g[:, h, V_COLS:HID, :], in_=src[:, V_COLS:HID, :])
+
         nc.vector.tensor_copy(out=bias_f, in_=bias_raw)
-        f_transpose(0, ps_y, "y", True)
-        w1_quantise(0)
         bias_ps = ps_y.tile([P, P], F32, tag="y")
         nc.tensor.transpose(bias_ps, bias_f, ident)
-        f_quantise(0)
         nc.vector.tensor_copy(out=bias_sb, in_=bias_ps[:, 0:8])
+        nc.vector.tensor_scalar_mul(out=b2_neg, in0=bias_sb[:, 4:8], scalar1=NEG - 1.0)
+        f_transpose(0, ps_y, "y", True)
+        w1_regroup(0)
+        f_quantise(0)
+        w1_quantise(0)
         stage1_matmuls(0, 0, ps_y, "y")
+        w1_regroup(1)
+        stage1_u(0)
         w1_quantise(1)
         stage1_matmuls(0, 1, ps_y, "y")
-        stage1_u(0)
         stage1_w(0)
-        nc.vector.tensor_scalar_mul(out=b2_neg, in0=bias_sb[:, 4:8], scalar1=NEG - 1.0)
         nc.scalar.copy(out=w2g, in_=w2_raw.rearrange("p t n -> p n t"))
         for pair in (1, 2, 3):
             f_transpose(pair, ps_t, "t", False)
@@ -232,13 +246,11 @@ def tile_nonlocalmp_pa_kernel(tc, F, W1, b1, W2, b2, out):
             phase = it % GROUPS_PER_CHUNK
             prefetch = nxt < N_CHUNKS
             if have_h:
-                pair_sum(g_h, 0)
+                pair_sum(g_h)
             if prefetch and phase == 2:
                 stage1_u(nxt)
-            if have_t:
+            if have_t and g_t < FIRST_SINGLE:
                 vector_e(g_t, N_E_VECTOR)
-            if have_h:
-                pair_sum(g_h, 1)
             if have_y and g_y > 0:
                 hidden_quantise(g_y)
             if it in (1, 2, 3):
@@ -255,7 +267,9 @@ def tile_nonlocalmp_pa_kernel(tc, F, W1, b1, W2, b2, out):
                 for s in range(4):
                     stage2_matmul(g_y, s)
                 for s in range(4):
-                    output_z(g_y, s, s >= N_E_VECTOR)
+                    output_z(g_y, s, s >= N_E_VECTOR and g_y < FIRST_SINGLE)
+                    if g_y >= FIRST_SINGLE:
+                        vector_lrelu(g_y, s)
             if prefetch and phase == 1:
                 stage1_matmuls(nxt, 0, ps_y, "y")
                 stage1_matmuls(nxt, 1, ps_y, "y")

@@ -47,11 +47,11 @@ def tile_nonlocalmp_pa_kernel(tc, F, W1, b1, W2, b2, out):
         w2_raw = const.tile([P, 4, Q], BF16)
         bias_raw = const.tile([P, P], BF16)
         nc.vector.memset(bias_raw, 0.0)
+        nc.sync.dma_start(out=bias_raw[0:4, :], in_=b1.rearrange("(r c) -> r c", c=P))
+        nc.sync.dma_start(out=bias_raw[4:8, :], in_=b2.rearrange("(r c) -> r c", c=P))
         nc.sync.dma_start(out=f_raw[:, 0:2, :], in_=f_view[:, 0:2, :])
-        nc.sync.dma_start(out=w1_dst[:, 0:2, :], in_=w1_view[:, 0:2, :])
         nc.sync.dma_start(out=w1_dst[:, 2:4, :], in_=w1_view[:, 2:4, :])
-        nc.scalar.dma_start(out=bias_raw[0:4, :], in_=b1.rearrange("(r c) -> r c", c=P))
-        nc.scalar.dma_start(out=bias_raw[4:8, :], in_=b2.rearrange("(r c) -> r c", c=P))
+        nc.sync.dma_start(out=w1_dst[:, 0:2, :], in_=w1_view[:, 0:2, :])
         nc.sync.dma_start(out=w2_raw, in_=W2.rearrange("(t p) n -> p t n", p=P))
         nc.sync.dma_start(out=f_raw[:, 2:8, :], in_=f_view[:, 2:8, :])
 
@@ -224,15 +224,15 @@ def tile_nonlocalmp_pa_kernel(tc, F, W1, b1, W2, b2, out):
         nc.vector.tensor_copy(out=bias_sb, in_=bias_ps[:, 0:8])
         nc.vector.tensor_scalar_mul(out=b2_neg, in0=bias_sb[:, 4:8], scalar1=NEG - 1.0)
         f_transpose(0, ps_y, "y", True)
-        w1_regroup(0)
-        f_quantise(0)
-        w1_quantise(0)
-        stage1_matmuls(0, 0, ps_y, "y")
         w1_regroup(1)
-        stage1_u(0)
+        f_quantise(0)
         w1_quantise(1)
         stage1_matmuls(0, 1, ps_y, "y")
+        w1_regroup(0)
         stage1_w(0)
+        w1_quantise(0)
+        stage1_matmuls(0, 0, ps_y, "y")
+        stage1_u(0)
         nc.scalar.copy(out=w2g, in_=w2_raw.rearrange("p t n -> p n t"))
         for pair in (1, 2, 3):
             f_transpose(pair, ps_t, "t", False)

@@ -70,7 +70,6 @@ def tile_nonlocalmp_pa_kernel(tc, F, W1, b1, W2, b2, out):
         w2_scales = const.tile([P, Q], U8, align_bytes=64)
         bias_f = const.tile([P, P], F32)
         bias_sb = const.tile([P, 8], F32)
-        b2_neg = const.tile([P, 4], F32)
 
         def f_transpose(pair, pool, tag, on_vector):
             ft = pool.tile([P, 2, 2, P], F32, tag=tag)
@@ -164,8 +163,8 @@ def tile_nonlocalmp_pa_kernel(tc, F, W1, b1, W2, b2, out):
             )
             y_tiles[(g, s)] = y_t
 
-        def output_z(g, s, scalar_makes_e):
-            if s == 0:
+        def output_z(g, s):
+            if s == 2:
                 z_new = work.tile([P, 4, 512], F32, tag="z")
                 e_new = work.tile([P, 4, 512], F32, tag="e")
                 z_tiles[g] = z_new
@@ -173,9 +172,10 @@ def tile_nonlocalmp_pa_kernel(tc, F, W1, b1, W2, b2, out):
             y_t = y_tiles[(g, s)]
             nc.scalar.activation(out=z_tiles[g][:, s, :], in_=y_t, func=ACT.Identity, scale=1.0,
                                  bias=bias_sb[:, 4 + s:5 + s])
-            if scalar_makes_e:
-                nc.scalar.activation(out=e_tiles[g][:, s, :], in_=y_t, func=ACT.Relu, scale=NEG - 1.0,
-                                     bias=b2_neg[:, s:s + 1])
+
+        def scalar_e(g):
+            nc.scalar.activation(out=e_tiles[g][:, N_E_VECTOR:4, :], in_=z_tiles[g][:, N_E_VECTOR:4, :],
+                                 func=ACT.Relu, scale=NEG - 1.0)
 
         def vector_lrelu(g, s):
             z_s = z_tiles[g][:, s, :]
@@ -222,7 +222,6 @@ def tile_nonlocalmp_pa_kernel(tc, F, W1, b1, W2, b2, out):
         bias_ps = ps_y.tile([P, P], F32, tag="y")
         nc.tensor.transpose(bias_ps, bias_f, ident)
         nc.vector.tensor_copy(out=bias_sb, in_=bias_ps[:, 0:8])
-        nc.vector.tensor_scalar_mul(out=b2_neg, in0=bias_sb[:, 4:8], scalar1=NEG - 1.0)
         f_transpose(0, ps_y, "y", True)
         w1_regroup(1)
         f_quantise(0)
@@ -264,12 +263,14 @@ def tile_nonlocalmp_pa_kernel(tc, F, W1, b1, W2, b2, out):
             if prefetch and phase == 2:
                 stage1_w(nxt)
             if have_y:
-                for s in range(4):
+                for s in (2, 3, 0, 1):
                     stage2_matmul(g_y, s)
-                for s in range(4):
-                    output_z(g_y, s, s >= N_E_VECTOR and g_y < FIRST_SINGLE)
+                for s in (2, 3, 0, 1):
+                    output_z(g_y, s)
                     if g_y >= FIRST_SINGLE:
                         vector_lrelu(g_y, s)
+                if g_y < FIRST_SINGLE:
+                    scalar_e(g_y)
             if prefetch and phase == 1:
                 stage1_matmuls(nxt, 0, ps_y, "y")
                 stage1_matmuls(nxt, 1, ps_y, "y")

@@ -23,9 +23,13 @@ N_GROUPS = B // GROUP_B
 CHUNK_B = 8
 GROUPS_PER_CHUNK = CHUNK_B // GROUP_B
 N_CHUNKS = B // CHUNK_B
+EARLY_GROUPS = 2
 FIRST_SINGLE = N_GROUPS - 2
 V_COLS = 320
-N_E_VECTOR = 2
+
+
+def n_e_vector(g):
+    return 0 if g < EARLY_GROUPS else 2
 
 
 def tile_nonlocalmp_pa_kernel(tc, F, W1, b1, W2, b2, out):
@@ -36,8 +40,7 @@ def tile_nonlocalmp_pa_kernel(tc, F, W1, b1, W2, b2, out):
         ctx.enter_context(tc.manual_schedule())
         const = ctx.enter_context(tc.tile_pool(name="const", bufs=1))
         work = ctx.enter_context(tc.tile_pool(name="work", bufs=3))
-        ps_y = ctx.enter_context(tc.psum_pool(name="ps_y", bufs=4))
-        ps_t = ctx.enter_context(tc.psum_pool(name="ps_t", bufs=4))
+        ring = ctx.enter_context(tc.psum_pool(name="ring", bufs=8))
 
         w1_raw = const.tile([P, 8, HID], BF16)
         w1_view = W1.rearrange("(g q e) c -> q g (e c)", g=4, q=P, e=2)
@@ -89,11 +92,13 @@ def tile_nonlocalmp_pa_kernel(tc, F, W1, b1, W2, b2, out):
             nc.vector.quantize_mx(out=f_codes[:, rows].bitcast(FP8X4), scales=f_scales[:, rows],
                                   in_=fg[:, 1024 * pair:1024 * (pair + 1)])
 
-        def w1_quantise(h):
+        def w1_quantise(h, half):
+            c0 = HID // 2 * half
+            cols = slice(HID * h + c0, HID * h + c0 + HID // 2)
             nc.vector.quantize_mx(
-                out=w1_codes[:, HID * h:HID * (h + 1)].bitcast(FP8X4),
-                scales=w1_scales[:, HID * h:HID * (h + 1)],
-                in_=w1g[:, h].rearrange("q c t -> q (c t)"),
+                out=w1_codes[:, cols].bitcast(FP8X4),
+                scales=w1_scales[:, cols],
+                in_=w1g[:, h, c0:c0 + HID // 2].rearrange("q c t -> q (c t)"),
             )
 
         b1_bc = bias_sb[:, 0:4].unsqueeze(1).to_broadcast([P, P, 4])
@@ -154,7 +159,7 @@ def tile_nonlocalmp_pa_kernel(tc, F, W1, b1, W2, b2, out):
         def stage2_matmul(g, s):
             m = slice(P * s, P * (s + 1))
             h_codes, h_scales = code_tiles[g]
-            y_t = ps_y.tile([P, 512], F32, tag="y")
+            y_t = ring.tile([P, 512], F32, tag="y")
             nc.tensor.matmul_mx(
                 out=y_t,
                 lhsT=w2_codes[:, m].bitcast(FP8X4), lhsT_scale=w2_scales[:, m],
@@ -174,7 +179,8 @@ def tile_nonlocalmp_pa_kernel(tc, F, W1, b1, W2, b2, out):
                                  bias=bias_sb[:, 4 + s:5 + s])
 
         def scalar_e(g):
-            nc.scalar.activation(out=e_tiles[g][:, N_E_VECTOR:4, :], in_=z_tiles[g][:, N_E_VECTOR:4, :],
+            first = n_e_vector(g)
+            nc.scalar.activation(out=e_tiles[g][:, first:4, :], in_=z_tiles[g][:, first:4, :],
                                  func=ACT.Relu, scale=NEG - 1.0)
 
         def vector_lrelu(g, s):
@@ -187,7 +193,7 @@ def tile_nonlocalmp_pa_kernel(tc, F, W1, b1, W2, b2, out):
                                     scalar1=NEG - 1.0, scalar2=0.0, op0=ALU.mult, op1=ALU.max)
 
         def back_transpose(g, n):
-            tr = ps_t.tile([P, Q], F32, tag="t")
+            tr = ring.tile([P, Q], F32, tag="y")
             c = slice(P * n, P * (n + 1))
             for s in range(4):
                 m = slice(P * s, P * (s + 1))
@@ -213,28 +219,33 @@ def tile_nonlocalmp_pa_kernel(tc, F, W1, b1, W2, b2, out):
                 in_=o_tiles[g][:, n0:n1, :],
             )
 
+        def regroup(copy, dst, src):
+            copy(out=dst.rearrange("p (c i) t -> p c t i", i=4), in_=src.rearrange("p t (c i) -> p c t i", i=4))
+
         def w1_regroup(h):
-            src = w1_raw[:, 4 * h:4 * h + 4, :].rearrange("q t c -> q c t")
-            nc.vector.tensor_copy(out=w1g[:, h, 0:V_COLS, :], in_=src[:, 0:V_COLS, :])
-            nc.scalar.copy(out=w1g[:, h, V_COLS:HID, :], in_=src[:, V_COLS:HID, :])
+            src = w1_raw[:, 4 * h:4 * h + 4, :]
+            regroup(nc.vector.tensor_copy, w1g[:, h, 0:V_COLS, :], src[:, :, 0:V_COLS])
+            regroup(nc.scalar.copy, w1g[:, h, V_COLS:HID, :], src[:, :, V_COLS:HID])
 
         nc.vector.tensor_copy(out=bias_f, in_=bias_raw)
-        bias_ps = ps_y.tile([P, P], F32, tag="y")
+        bias_ps = ring.tile([P, P], F32, tag="y")
         nc.tensor.transpose(bias_ps, bias_f, ident)
         nc.vector.tensor_copy(out=bias_sb, in_=bias_ps[:, 0:8])
-        f_transpose(0, ps_y, "y", True)
+        f_transpose(0, ring, "y", False)
         w1_regroup(1)
         f_quantise(0)
-        w1_quantise(1)
-        stage1_matmuls(0, 1, ps_y, "y")
+        w1_quantise(1, 0)
         w1_regroup(0)
+        w1_quantise(1, 1)
+        stage1_matmuls(0, 1, ring, "y")
         stage1_w(0)
-        w1_quantise(0)
-        stage1_matmuls(0, 0, ps_y, "y")
+        w1_quantise(0, 0)
+        w1_quantise(0, 1)
+        stage1_matmuls(0, 0, ring, "y")
         stage1_u(0)
-        nc.scalar.copy(out=w2g, in_=w2_raw.rearrange("p t n -> p n t"))
+        regroup(nc.scalar.copy, w2g, w2_raw)
         for pair in (1, 2, 3):
-            f_transpose(pair, ps_t, "t", False)
+            f_transpose(pair, ring, "y", False)
 
         for it in range(N_GROUPS + 2):
             g_h, g_y, g_t = it, it - 1, it - 2
@@ -248,10 +259,10 @@ def tile_nonlocalmp_pa_kernel(tc, F, W1, b1, W2, b2, out):
                 pair_sum(g_h)
             if prefetch and phase == 2:
                 stage1_u(nxt)
-            if have_t and g_t < FIRST_SINGLE:
-                vector_e(g_t, N_E_VECTOR)
-            if have_y and g_y > 0:
+            if 0 < g_y < N_GROUPS - 1:
                 hidden_quantise(g_y)
+            if have_t and g_t < FIRST_SINGLE and n_e_vector(g_t) > 0:
+                vector_e(g_t, n_e_vector(g_t))
             if it in (1, 2, 3):
                 f_quantise(it)
             if have_h:
@@ -260,6 +271,8 @@ def tile_nonlocalmp_pa_kernel(tc, F, W1, b1, W2, b2, out):
                 nc.vector.quantize_mx(out=w2_codes.bitcast(FP8X4), scales=w2_scales,
                                       in_=w2g.rearrange("p n t -> p (n t)"))
                 hidden_quantise(0)
+            if g_h == N_GROUPS - 1:
+                hidden_quantise(g_h)
             if prefetch and phase == 2:
                 stage1_w(nxt)
             if have_y:
@@ -272,13 +285,13 @@ def tile_nonlocalmp_pa_kernel(tc, F, W1, b1, W2, b2, out):
                 if g_y < FIRST_SINGLE:
                     scalar_e(g_y)
             if prefetch and phase == 1:
-                stage1_matmuls(nxt, 0, ps_y, "y")
-                stage1_matmuls(nxt, 1, ps_y, "y")
+                stage1_matmuls(nxt, 0, ring, "y")
+                stage1_matmuls(nxt, 1, ring, "y")
             if have_t:
                 for n in range(4):
                     back_transpose(g_t, n)
                 for n in range(4):
-                    copy_out(g_t, n, (not have_h) and n % 2 == 1)
+                    copy_out(g_t, n, g_h >= N_GROUPS - 1 and n % 2 == 1)
                     if g_t >= N_GROUPS - 2:
                         store(g_t, n, n + 1)
                 if g_t < N_GROUPS - 2:

from contextlib import ExitStack

import concourse.mybir as mybir
from concourse.masks import make_identity

F32 = mybir.dt.float32
BF16 = mybir.dt.bfloat16
U32 = mybir.dt.uint32
U8 = mybir.dt.uint8
FP8X4 = mybir.dt.float8_e4m3fn_x4
ALU = mybir.AluOpType
ACT = mybir.ActivationFunctionType

P = 128
B, V, D, HID, Q = 64, 16, 512, 512, 512
ROWS1 = B * V
PAIRS = V * V
NEG = 0.2
FLOPS = 2 * ROWS1 * 2 * D * HID + 2 * B * PAIRS * HID * Q

GROUP_B = 2
N_GROUPS = B // GROUP_B
CHUNK_B = 8
GROUPS_PER_CHUNK = CHUNK_B // GROUP_B
N_CHUNKS = B // CHUNK_B
EARLY_GROUPS = 2
FIRST_SINGLE = N_GROUPS - 2
V_COLS = 320


def n_e_vector(g):
    return 0 if g < EARLY_GROUPS else 2


def tile_nonlocalmp_pa_kernel(tc, F, W1, b1, W2, b2, out):
    nc = tc.nc
    f_flat = F.flatten_outer_dims()
    out_flat = out.flatten_outer_dims()
    with ExitStack() as ctx:
        ctx.enter_context(tc.manual_schedule())
        const = ctx.enter_context(tc.tile_pool(name="const", bufs=1))
        work = ctx.enter_context(tc.tile_pool(name="work", bufs=3))
        ring = ctx.enter_context(tc.psum_pool(name="ring", bufs=8))

        w1_raw = const.tile([P, 8, HID], BF16)
        w1_view = W1.rearrange("(g q e) c -> q g (e c)", g=4, q=P, e=2)
        w1_dst = w1_raw.rearrange("q (g e) c -> q g (e c)", e=2)
        f_raw = const.tile([P, 8, D], BF16)
        f_view = f_flat.rearrange("(n p) d -> p n d", p=P)
        w2_raw = const.tile([P, 4, Q], BF16)
        bias_raw = const.tile([P, P], BF16)
        nc.vector.memset(bias_raw, 0.0)
        nc.sync.dma_start(out=bias_raw[0:4, :], in_=b1.rearrange("(r c) -> r c", c=P))
        nc.sync.dma_start(out=bias_raw[4:8, :], in_=b2.rearrange("(r c) -> r c", c=P))
        nc.sync.dma_start(out=f_raw[:, 0:2, :], in_=f_view[:, 0:2, :])
        nc.sync.dma_start(out=w1_dst[:, 2:4, :], in_=w1_view[:, 2:4, :])
        nc.sync.dma_start(out=w1_dst[:, 0:2, :], in_=w1_view[:, 0:2, :])
        nc.sync.dma_start(out=w2_raw, in_=W2.rearrange("(t p) n -> p t n", p=P))
        nc.sync.dma_start(out=f_raw[:, 2:8, :], in_=f_view[:, 2:8, :])

        ident = const.tile([P, P], F32)
        make_identity(nc, ident)

        fg = const.tile([P, ROWS1 * 4], BF16, align_bytes=64)
        fg_w = fg.bitcast(F32).rearrange("p (r u) -> p r u", u=2)
        f_codes = const.tile([P, ROWS1], U32, align_bytes=64)
        f_scales = const.tile([P, ROWS1], U8, align_bytes=64)
        w1g = const.tile([P, 2, HID, 4], BF16, align_bytes=64)
        w1_codes = const.tile([P, 2 * HID], U32, align_bytes=64)
        w1_scales = const.tile([P, 2 * HID], U8, align_bytes=64)
        w2g = const.tile([P, Q, 4], BF16, align_bytes=64)
        w2_codes = const.tile([P, Q], U32, align_bytes=64)
        w2_scales = const.tile([P, Q], U8, align_bytes=64)
        bias_f = const.tile([P, P], F32)
        bias_sb = const.tile([P, 8], F32)

        def f_transpose(pair, pool, tag, on_vector):
            ft = pool.tile([P, 2, 2, P], F32, tag=tag)
            for nn in range(2):
                words = f_raw[:, 2 * pair + nn, :].bitcast(F32)
                for u in range(2):
                    nc.tensor.transpose(ft[:, nn, u, :], words[:, P * u:P * (u + 1)], ident)
            dst = fg_w[:, 256 * pair:256 * (pair + 1), :].rearrange("p (n r) u -> p n r u", n=2)
            src = ft.rearrange("p n u r -> p n r u")
            if on_vector:
                nc.vector.tensor_copy(out=dst, in_=src)
            else:
                nc.scalar.copy(out=dst, in_=src)

        def f_quantise(pair):
            rows = slice(256 * pair, 256 * (pair + 1))
            nc.vector.quantize_mx(out=f_codes[:, rows].bitcast(FP8X4), scales=f_scales[:, rows],
                                  in_=fg[:, 1024 * pair:1024 * (pair + 1)])

        def w1_quantise(h, half):
            c0 = HID // 2 * half
            cols = slice(HID * h + c0, HID * h + c0 + HID // 2)
            nc.vector.quantize_mx(
                out=w1_codes[:, cols].bitcast(FP8X4),
                scales=w1_scales[:, cols],
                in_=w1g[:, h, c0:c0 + HID // 2].rearrange("q c t -> q (c t)"),
            )

        b1_bc = bias_sb[:, 0:4].unsqueeze(1).to_broadcast([P, P, 4])
        s1_banks, u_tiles, w_tiles = {}, {}, {}
        a_tiles, h_tiles, code_tiles = {}, {}, {}
        y_tiles, z_tiles, e_tiles, t_tiles, o_tiles = {}, {}, {}, {}, {}

        def stage1_matmuls(chunk, h, pool, tag):
            cols = slice(P * chunk, P * (chunk + 1))
            bank = pool.tile([P, 4, P], F32, tag=tag)
            for t in range(4):
                m = slice(HID * h + P * t, HID * h + P * (t + 1))
                nc.tensor.matmul_mx(
                    out=bank[:, t, :],
                    lhsT=w1_codes[:, m].bitcast(FP8X4), lhsT_scale=w1_scales[:, m],
                    rhs=f_codes[:, cols].bitcast(FP8X4), rhs_scale=f_scales[:, cols],
                    start=True, stop=True,
                )
            s1_banks[(chunk, h)] = bank

        def stage1_u(chunk):
            u_sb = work.tile([P, P, 4], F32, tag="usb", bufs=2)
            nc.vector.tensor_tensor(out=u_sb, in0=s1_banks[(chunk, 0)].rearrange("p t r -> p r t"), in1=b1_bc,
                                    op=ALU.add)
            u_tiles[chunk] = u_sb

        def stage1_w(chunk):
            w_sb = work.tile([P, P, 4], F32, tag="wsb", bufs=2)
            nc.scalar.copy(out=w_sb, in_=s1_banks[(chunk, 1)].rearrange("p t r -> p r t"))
            w_tiles[chunk] = w_sb

        def pair_sum(g):
            a_new = work.tile([P, GROUP_B, V, V, 4], F32, tag="a")
            a_tiles[g] = a_new
            chunk = g // GROUPS_PER_CHUNK
            r0 = V * ((g * GROUP_B) % CHUNK_B)
            rows = slice(r0, r0 + GROUP_B * V)
            full = [P, GROUP_B, V, V, 4]
            nc.vector.tensor_tensor(
                out=a_new,
                in0=w_tiles[chunk][:, rows, :].rearrange("p (b j) t -> p b j t", b=GROUP_B).unsqueeze(2).to_broadcast(full),
                in1=u_tiles[chunk][:, rows, :].rearrange("p (b i) t -> p b i t", b=GROUP_B).unsqueeze(3).to_broadcast(full),
                op=ALU.add,
            )

        def hidden_lrelu(g):
            a_flat = a_tiles[g].rearrange("p b i j t -> p (b i j t)")
            h_t = work.tile([P, GROUP_B * PAIRS * 4], BF16, tag="h", align_bytes=64)
            nc.vector.scalar_tensor_tensor(out=h_t, in0=a_flat, scalar=NEG, in1=a_flat, op0=ALU.mult, op1=ALU.max)
            h_tiles[g] = h_t

        def hidden_quantise(g):
            h_codes = work.tile([P, GROUP_B * PAIRS], U32, tag="hc", align_bytes=64)
            h_scales = work.tile([P, GROUP_B * PAIRS], U8, tag="hs", align_bytes=64)
            nc.vector.quantize_mx(out=h_codes.bitcast(FP8X4), scales=h_scales, in_=h_tiles[g])
            code_tiles[g] = (h_codes, h_scales)

        def stage2_matmul(g, s):
            m = slice(P * s, P * (s + 1))
            h_codes, h_scales = code_tiles[g]
            y_t = ring.tile([P, 512], F32, tag="y")
            nc.tensor.matmul_mx(
                out=y_t,
                lhsT=w2_codes[:, m].bitcast(FP8X4), lhsT_scale=w2_scales[:, m],
                rhs=h_codes.bitcast(FP8X4), rhs_scale=h_scales,
                start=True, stop=True,
            )
            y_tiles[(g, s)] = y_t

        def output_z(g, s):
            if s == 2:
                z_new = work.tile([P, 4, 512], F32, tag="z")
                e_new = work.tile([P, 4, 512], F32, tag="e")
                z_tiles[g] = z_new
                e_tiles[g] = e_new
            y_t = y_tiles[(g, s)]
            nc.scalar.activation(out=z_tiles[g][:, s, :], in_=y_t, func=ACT.Identity, scale=1.0,
                                 bias=bias_sb[:, 4 + s:5 + s])

        def scalar_e(g):
            first = n_e_vector(g)
            nc.scalar.activation(out=e_tiles[g][:, first:4, :], in_=z_tiles[g][:, first:4, :],
                                 func=ACT.Relu, scale=NEG - 1.0)

        def vector_lrelu(g, s):
            z_s = z_tiles[g][:, s, :]
            nc.vector.scalar_tensor_tensor(out=e_tiles[g][:, s, :], in0=z_s, scalar=NEG, in1=z_s,
                                           op0=ALU.mult, op1=ALU.max)

        def vector_e(g, n_slices):
            nc.vector.tensor_scalar(out=e_tiles[g][:, 0:n_slices, :], in0=z_tiles[g][:, 0:n_slices, :],
                                    scalar1=NEG - 1.0, scalar2=0.0, op0=ALU.mult, op1=ALU.max)

        def back_transpose(g, n):
            tr = ring.tile([P, Q], F32, tag="y")
            c = slice(P * n, P * (n + 1))
            for s in range(4):
                m = slice(P * s, P * (s + 1))
                if g < FIRST_SINGLE:
                    nc.tensor.matmul(out=tr[:, m], lhsT=z_tiles[g][:, s, c], rhs=ident, is_transpose=True,
                                     start=True, stop=False)
                nc.tensor.matmul(out=tr[:, m], lhsT=e_tiles[g][:, s, c], rhs=ident, is_transpose=True,
                                 start=(g >= FIRST_SINGLE), stop=True)
            t_tiles[(g, n)] = tr

        def copy_out(g, n, on_vector):
            if n == 0:
                o_new = work.tile([P, 4, Q], F32, tag="o")
                o_tiles[g] = o_new
            if on_vector:
                nc.vector.tensor_copy(out=o_tiles[g][:, n, :], in_=t_tiles[(g, n)])
            else:
                nc.scalar.copy(out=o_tiles[g][:, n, :], in_=t_tiles[(g, n)])

        def store(g, n0, n1):
            nc.sync.dma_start(
                out=out_flat[512 * g + P * n0:512 * g + P * n1, :].rearrange("(n p) q -> p n q", p=P),
                in_=o_tiles[g][:, n0:n1, :],
            )

        def regroup(copy, dst, src):
            copy(out=dst.rearrange("p (c i) t -> p c t i", i=4), in_=src.rearrange("p t (c i) -> p c t i", i=4))

        def w1_regroup(h):
            src = w1_raw[:, 4 * h:4 * h + 4, :]
            regroup(nc.vector.tensor_copy, w1g[:, h, 0:V_COLS, :], src[:, :, 0:V_COLS])
            regroup(nc.scalar.copy, w1g[:, h, V_COLS:HID, :], src[:, :, V_COLS:HID])

        nc.vector.tensor_copy(out=bias_f, in_=bias_raw)
        bias_ps = ring.tile([P, P], F32, tag="y")
        nc.tensor.transpose(bias_ps, bias_f, ident)
        nc.vector.tensor_copy(out=bias_sb, in_=bias_ps[:, 0:8])
        f_transpose(0, ring, "y", False)
        w1_regroup(1)
        f_quantise(0)
        w1_quantise(1, 0)
        w1_regroup(0)
        w1_quantise(1, 1)
        stage1_matmuls(0, 1, ring, "y")
        stage1_w(0)
        w1_quantise(0, 0)
        w1_quantise(0, 1)
        stage1_matmuls(0, 0, ring, "y")
        stage1_u(0)
        regroup(nc.scalar.copy, w2g, w2_raw)
        for pair in (1, 2, 3):
            f_transpose(pair, ring, "y", False)

        for it in range(N_GROUPS + 2):
            g_h, g_y, g_t = it, it - 1, it - 2
            have_h = g_h < N_GROUPS
            have_y = 0 <= g_y < N_GROUPS
            have_t = 0 <= g_t
            nxt = it // GROUPS_PER_CHUNK + 1
            phase = it % GROUPS_PER_CHUNK
            prefetch = nxt < N_CHUNKS
            if have_h:
                pair_sum(g_h)
            if prefetch and phase == 2:
                stage1_u(nxt)
            if 0 < g_y < N_GROUPS - 1:
                hidden_quantise(g_y)
            if have_t and g_t < FIRST_SINGLE and n_e_vector(g_t) > 0:
                vector_e(g_t, n_e_vector(g_t))
            if it in (1, 2, 3):
                f_quantise(it)
            if have_h:
                hidden_lrelu(g_h)
            if it == 0:
                nc.vector.quantize_mx(out=w2_codes.bitcast(FP8X4), scales=w2_scales,
                                      in_=w2g.rearrange("p n t -> p (n t)"))
                hidden_quantise(0)
            if g_h == N_GROUPS - 1:
                hidden_quantise(g_h)
            if prefetch and phase == 2:
                stage1_w(nxt)
            if have_y:
                for s in (2, 3, 0, 1):
                    stage2_matmul(g_y, s)
                for s in (2, 3, 0, 1):
                    output_z(g_y, s)
                    if g_y >= FIRST_SINGLE:
                        vector_lrelu(g_y, s)
                if g_y < FIRST_SINGLE:
                    scalar_e(g_y)
            if prefetch and phase == 1:
                stage1_matmuls(nxt, 0, ring, "y")
                stage1_matmuls(nxt, 1, ring, "y")
            if have_t:
                for n in range(4):
                    back_transpose(g_t, n)
                for n in range(4):
                    copy_out(g_t, n, g_h >= N_GROUPS - 1 and n % 2 == 1)
                    if g_t >= N_GROUPS - 2:
                        store(g_t, n, n + 1)
                if g_t < N_GROUPS - 2:
                    store(g_t, 0, 4)
